import numpy as np
import ml_dtypes


BF16 = ml_dtypes.bfloat16


def bf(x):
    return np.asarray(x, np.float32).astype(BF16)


def f64(x):
    return np.asarray(x).astype(np.float64)


E2M1 = np.array([0.0, 0.5, 1.0, 1.5, 2.0, 3.0, 4.0, 6.0, -0.0, -0.5, -1.0, -1.5, -2.0, -3.0, -4.0, -6.0])


def pack_weight(w, fmt):
    k, n = w.shape
    w = f64(bf(w)).reshape(k // 32, 32, n)
    amax = np.abs(w).max(1)
    if fmt == "e4m3":
        byte = np.frexp(amax)[1] - 1 + 127 - 7
    else:
        mant, ex = np.frexp(amax / 6.0)
        byte = np.where(mant > 0.5, ex, ex - 1) + 127
    byte = np.clip(np.where(amax > 0, byte, 1), 1, 254)
    scaled = (w * np.exp2(127.0 - byte)[:, None, :]).reshape(k, n).astype(np.float32)
    by_word = np.ascontiguousarray(scaled.reshape(k // 512, 128, 4, n).transpose(0, 1, 3, 2))
    if fmt == "e4m3":
        words = by_word.astype(ml_dtypes.float8_e4m3fn).view(np.uint8)
    else:
        c = by_word.astype(ml_dtypes.float4_e2m1fn).view(np.uint8) & 0xF
        words = c[..., 0::2] | (c[..., 1::2] << 4)
    return np.ascontiguousarray(words), np.ascontiguousarray(byte.astype(np.uint8).reshape(k // 512, 16, n))


def unpack_weight(words, scales, fmt):
    g, p, n, _ = words.shape
    if fmt == "e4m3":
        vals = np.ascontiguousarray(words).view(ml_dtypes.float8_e4m3fn).astype(np.float64)
    else:
        nib = np.empty((g, p, n, 4), np.uint8)
        nib[..., 0::2] = words & 0xF
        nib[..., 1::2] = words >> 4
        vals = E2M1[nib]
    vals = vals * np.repeat(np.exp2(scales.astype(np.float64) - 127.0), 8, axis=1)[..., None]
    return vals.transpose(0, 1, 3, 2).reshape(g * 512, n)

def pack4(w):
    words, scales = pack_weight(w, "e2m1")
    return words.reshape(words.shape[0], 128, -1), scales


def unpack4(words, scales):
    return unpack_weight(words.reshape(words.shape[0], 128, -1, 2), scales, "e2m1")


def kspread(k):
    return np.exp2(np.repeat(np.random.randint(-6, 7, k // 32), 32).astype(np.float64))


B, D, H = 1536, 2048, 1536


def sigmoid(v):
    return 1.0 / (1.0 + np.exp(-v))


def setup_inputs():
    s = kspread(D)
    x = np.random.standard_normal((B, D)) * s
    x_words, x_scales = pack4(np.ascontiguousarray(x.T))
    w = np.random.standard_normal((4 * H, D)) * 1.5 / np.sqrt(D) / s[None, :]
    words, scales = pack4(np.ascontiguousarray(w.T))
    b_ih0 = bf(np.random.standard_normal(4 * H) * 0.3)
    b_hh0 = bf(np.random.standard_normal(4 * H) * 0.3)
    return {"x_words": x_words,
            "x_scales": x_scales,
            "W_ih0_words": words,
            "W_ih0_scales": scales,
            "b_ih0": b_ih0,
            "b_hh0": b_hh0}


def reference(x_words, x_scales, W_ih0_words, W_ih0_scales, b_ih0, b_hh0):
    wt = unpack4(W_ih0_words, W_ih0_scales)
    b = f64(b_ih0) + f64(b_hh0)
    xq = unpack4(x_words, x_scales).T
    a_i = (xq @ wt[:, :H]) + b[:H]
    a_go = (xq @ wt[:, 2 * H:]) + b[2 * H:]
    a_g, a_o = a_go[:, :H], a_go[:, H:]
    c = sigmoid(a_i) * np.tanh(a_g)
    return sigmoid(a_o) * np.tanh(c)

@@ -1,0 +1,288 @@
+from contextlib import ExitStack
+
+import concourse.mybir as mybir
+
+TOKENS, K, H = 1536, 2048, 1536
+
+P = 128
+K_PASS = 512
+PASSES = K // K_PASS
+X_CODE_PARTS = ((0, 256), (256, 768), (768, 1536))
+X_PLANE_PARTS = ((0, 768), (768, 1536))
+W_PARTS = ((0, 512), (512, 1536))
+N_TILE = 512
+BLOCKS = H // N_TILE
+GATES = (0, 2, 3)
+TOKEN_TILES = TOKENS // P
+QUADRANT = 32
+
+FLOPS = 2 * TOKENS * K * len(GATES) * H
+BYTES = (
+    K * TOKENS // 2 + K // 32 * TOKENS
+    + K * len(GATES) * H // 2 + K // 32 * len(GATES) * H
+    + 2 * 2 * len(GATES) * H
+    + 4 * TOKENS * H
+)
+
+F32 = mybir.dt.float32
+BF16 = mybir.dt.bfloat16
+I32 = mybir.dt.int32
+U8 = mybir.dt.uint8
+FP4X4 = mybir.dt.float4_e2m1fn_x4
+ADD = mybir.AluOpType.add
+MULT = mybir.AluOpType.mult
+SIGMOID = mybir.ActivationFunctionType.Sigmoid
+TANH = mybir.ActivationFunctionType.Tanh
+
+
+def load_codes(nc, codes, words, first_column, passes):
+    width = codes.shape[2]
+    source = words[passes.start : passes.stop, :, 2 * first_column : 2 * first_column + width]
+    nc.sync.dma_start(
+        out=codes[:, passes.start : passes.stop, :].bitcast(I32),
+        in_=source.rearrange("g p n -> p g n").bitcast(I32),
+    )
+
+
+def load_scales(nc, planes, scales, first_column):
+    width = planes.shape[2]
+    for q in range(4):
+        source = scales[:, 4 * q : 4 * q + 4, first_column : first_column + width]
+        nc.sync.dma_start(
+            out=planes[QUADRANT * q : QUADRANT * q + 4, :, :].bitcast(I32),
+            in_=source.rearrange("g r n -> r g n").bitcast(I32),
+        )
+
+
+def part_of(tiles, parts, column):
+    for tile, (start, stop) in zip(tiles, parts):
+        if start <= column < stop:
+            return tile, column - start
+
+
+def tile_lstmbaseline_pa_kernel(tc, x_words, x_scales, w_words, w_scales, b_ih, b_hh, out):
+    nc = tc.nc
+    with ExitStack() as ctx:
+        keep = ctx.enter_context(tc.tile_pool(name="keep", bufs=1))
+        work = ctx.enter_context(tc.tile_pool(name="work", bufs=3))
+        psum = ctx.enter_context(tc.psum_pool(name="psum", bufs=8))
+        ctx.enter_context(tc.manual_schedule())
+
+        def codes_tile(label, columns):
+            return keep.tile([P, PASSES, 2 * columns], U8, align_bytes=256, name=label + "_codes")
+
+        def planes_tile(label, columns):
+            return keep.tile([P, PASSES, columns], U8, align_bytes=256, name=label + "_planes")
+
+        x_codes = [codes_tile("x%d" % s, stop - start) for s, (start, stop) in enumerate(X_CODE_PARTS)]
+        x_planes = [planes_tile("x%d" % s, stop - start) for s, (start, stop) in enumerate(X_PLANE_PARTS)]
+        w_codes = [[codes_tile("w%d%d" % (j, s), b - a) for s, (a, b) in enumerate(W_PARTS)] for j in range(3)]
+        w_planes = [[planes_tile("w%d%d" % (j, s), b - a) for s, (a, b) in enumerate(W_PARTS)] for j in range(3)]
+
+        bias_rows = keep.tile([P, 2, N_TILE], BF16, name="bias_rows")
+        ones = keep.tile([P, len(GATES), P], BF16, name="ones")
+        bias_head = keep.tile([P, len(GATES), N_TILE], F32, name="bias_head")
+        bias_rest = keep.tile([P, len(GATES), H - N_TILE], F32, name="bias_rest")
+        spread = [keep.tile([P, len(GATES), H - N_TILE], BF16, name="spread%d" % s) for s in range(2)]
+        warm = keep.tile([P, 1], F32, name="warm")
+
+        nc.vector.memset(x_planes[0][:].bitcast(I32), 0)
+        nc.vector.memset(w_planes[0][0][:].bitcast(I32), 0)
+        nc.vector.memset(warm[:], 0.0)
+        nc.vector.memset(w_planes[1][0][:].bitcast(I32), 0)
+        nc.vector.memset(w_planes[2][0][:].bitcast(I32), 0)
+        nc.vector.memset(x_planes[1][:].bitcast(I32), 0)
+
+        nc.gpsimd.memset(bias_rows[:].rearrange("p s n -> p (s n)").bitcast(F32), 0.0)
+        for s, vector in enumerate((b_ih, b_hh)):
+            rows = vector.rearrange("(g n) -> g n", g=4)
+            nc.scalar.dma_start(out=bias_rows[0:P:QUADRANT, s, :], in_=rows[:, 0:N_TILE])
+        nc.scalar.activation(warm[:], warm[:], SIGMOID)
+        nc.gpsimd.memset(ones[:], 0.0)
+        for j, gate in enumerate(GATES):
+            nc.gpsimd.memset(ones[QUADRANT * gate : QUADRANT * (gate + 1), j, :], 1.0)
+        nc.gpsimd.memset(bias_rows[QUADRANT : 2 * QUADRANT, :, :].rearrange("p s n -> p (s n)").bitcast(F32), 0.0)
+        for j in range(len(GATES)):
+            nc.gpsimd.memset(w_planes[j][1][:].bitcast(F32), 0.0)
+
+        first, others = range(0, 1), range(1, PASSES)
+        load_codes(nc, w_codes[0][0], w_words, GATES[0] * H, first)
+        load_codes(nc, x_codes[0], x_words, 0, first)
+        load_scales(nc, x_planes[0], x_scales, 0)
+        load_scales(nc, w_planes[0][0], w_scales, GATES[0] * H)
+        load_codes(nc, x_codes[0], x_words, 0, others)
+        load_codes(nc, w_codes[0][0], w_words, GATES[0] * H, others)
+        for j in (1, 2):
+            load_scales(nc, w_planes[j][0], w_scales, GATES[j] * H)
+            load_codes(nc, w_codes[j][0], w_words, GATES[j] * H, range(PASSES))
+        load_codes(nc, x_codes[1], x_words, X_CODE_PARTS[1][0], range(PASSES))
+        load_scales(nc, x_planes[1], x_scales, X_PLANE_PARTS[1][0])
+        load_codes(nc, x_codes[2], x_words, X_CODE_PARTS[2][0], range(PASSES))
+        for j, gate in enumerate(GATES):
+            load_scales(nc, w_planes[j][1], w_scales, gate * H + N_TILE)
+            load_codes(nc, w_codes[j][1], w_words, gate * H + N_TILE, range(PASSES))
+        for j, gate in enumerate(GATES):
+            for s, vector in enumerate((b_ih, b_hh)):
+                nc.sync.dma_start(
+                    out=spread[s][:, j, :], in_=vector[gate * H + N_TILE : (gate + 1) * H].partition_broadcast(P)
+                )
+
+        for j in range(len(GATES)):
+            acc = psum.tile([P, N_TILE], F32, name="acc")
+            for s in range(2):
+                nc.tensor.matmul(
+                    out=acc[:], lhsT=ones[:, j, :], rhs=bias_rows[:, s, :], start=(s == 0), stop=(s == 1)
+                )
+            if j == 1:
+                nc.vector.tensor_copy(out=bias_head[:, j, :], in_=acc[:])
+            else:
+                nc.scalar.copy(bias_head[:, j, :], acc[:])
+
+        def bias(c, j, n0=0, n1=N_TILE):
+            if c == 0:
+                return bias_head[:, j, n0:n1]
+            first_column = (c - 1) * N_TILE
+            return bias_rest[:, j, first_column + n0 : first_column + n1]
+
+        def multiply(acc, t, c, j, g, column=0):
+            width = acc.shape[1]
+            x_code, m0 = part_of(x_codes, X_CODE_PARTS, P * t)
+            x_plane, m1 = part_of(x_planes, X_PLANE_PARTS, P * t)
+            w_code, n0 = part_of(w_codes[j], W_PARTS, N_TILE * c + column)
+            w_plane, n1 = part_of(w_planes[j], W_PARTS, N_TILE * c + column)
+            nc.tensor.matmul_mx(
+                out=acc[:],
+                lhsT=x_code[:, g, 2 * m0 : 2 * (m0 + P)].bitcast(FP4X4),
+                lhsT_scale=x_plane[:, g, m1 : m1 + P],
+                rhs=w_code[:, g, 2 * n0 : 2 * (n0 + width)].bitcast(FP4X4),
+                rhs_scale=w_plane[:, g, n1 : n1 + width],
+                start=(g == 0),
+                stop=(g == PASSES - 1),
+            )
+
+        def add_bias(out_ap, acc, c, j, n0=0, n1=N_TILE):
+            nc.vector.tensor_tensor(out=out_ap, in0=acc[:], in1=bias(c, j, n0, n1), op=ADD)
+
+        rest_sums = [(c, j) for c in range(1, BLOCKS) for j in range(len(GATES))]
+        pairs = [(c, t0) for c in range(BLOCKS) for t0 in range(0, TOKEN_TILES, 2)]
+
+        def gate_pair(c, t0, j):
+            accs = [psum.tile([P, N_TILE], F32, name="acc") for u in range(2)]
+            for g in range(PASSES):
+                for u in range(2):
+                    multiply(accs[u], t0 + u, c, j, g)
+            zj = work.tile([P, 2, N_TILE], F32, name="z%d" % j)
+            for u in range(2):
+                add_bias(zj[:, u, :], accs[u], c, j)
+            return zj
+
+        def squash(ap, j):
+            nc.scalar.activation(ap, ap, TANH if j == 1 else SIGMOID)
+
+        def multiply_into(engine, result, a, b):
+            engine.tensor_tensor(out=result, in0=a, in1=b, op=MULT)
+
+        def finish(c, t0, cell, out_gate):
+            hidden = work.tile([P, 2, N_TILE], F32, name="hidden")
+            multiply_into(nc.vector, hidden[:], out_gate[:], cell[:])
+            nc.sync.dma_start(
+                out=out[P * t0 : P * (t0 + 2), c * N_TILE : (c + 1) * N_TILE].rearrange("(u p) n -> p u n", p=P),
+                in_=hidden[:],
+            )
+
+        waiting = None
+        for c, t0 in pairs[:-2]:
+            in_gate = gate_pair(c, t0, 0)
+            squash(in_gate[:], 0)
+            if waiting:
+                squash(waiting[2][:], 1)
+            cell_gate = gate_pair(c, t0, 1)
+            squash(cell_gate[:], 1)
+            if waiting:
+                finish(*waiting)
+            cell = work.tile([P, 2, N_TILE], F32, name="cell")
+            multiply_into(nc.gpsimd, cell[:], in_gate[:], cell_gate[:])
+            out_gate = gate_pair(c, t0, 2)
+            squash(out_gate[:], 2)
+            waiting = (c, t0, cell, out_gate)
+            if t0 >= 4 and rest_sums:
+                bc, bj = rest_sums[0]
+                rest_sums = rest_sums[1:]
+                part = slice((bc - 1) * N_TILE, bc * N_TILE)
+                nc.gpsimd.tensor_tensor(
+                    out=bias_rest[:, bj, part], in0=spread[0][:, bj, part], in1=spread[1][:, bj, part], op=ADD
+                )
+
+        c, t0 = pairs[-2]
+        in_gate = gate_pair(c, t0, 0)
+        for u in range(2):
+            squash(in_gate[:, u, :], 0)
+        squash(waiting[2][:], 1)
+        cell_gate = gate_pair(c, t0, 1)
+        cell = work.tile([P, 2, N_TILE], F32, name="cell")
+        for u in range(2):
+            squash(cell_gate[:, u, :], 1)
+            multiply_into(nc.gpsimd, cell[:, u, :], in_gate[:, u, :], cell_gate[:, u, :])
+        finish(*waiting)
+        out_gate = gate_pair(c, t0, 2)
+        squash(cell[:, 0, :], 1)
+        for u in range(2):
+            squash(out_gate[:, u, :], 2)
+        hidden = work.tile([P, 2, N_TILE], F32, name="hidden")
+
+        def finish_half(u):
+            multiply_into(nc.gpsimd, hidden[:, u, :], out_gate[:, u, :], cell[:, u, :])
+            nc.sync.dma_start(
+                out=out[P * (t0 + u) : P * (t0 + u + 1), c * N_TILE : (c + 1) * N_TILE], in_=hidden[:, u, :]
+            )
+
+        t = TOKEN_TILES - 2
+
+        def single(t, j, n0, n1):
+            acc = psum.tile([P, n1 - n0], F32, name="acc")
+            for g in range(PASSES):
+                multiply(acc, t, c, j, g, n0)
+            piece = work.tile([P, n1 - n0], F32, name="piece%d" % j)
+            add_bias(piece[:], acc, c, j, n0, n1)
+            return piece
+
+        def product(engine, label, a, b):
+            result = work.tile([P, a.shape[1]], F32, name=label)
+            engine.tensor_tensor(out=result[:], in0=a, in1=b, op=MULT)
+            return result
+
+        def store(t, n0, n1, result):
+            nc.sync.dma_start(out=out[P * t : P * (t + 1), c * N_TILE + n0 : c * N_TILE + n1], in_=result[:])
+
+        y_i = single(t, 0, 0, N_TILE)
+        squash(y_i[:], 0)
+        finish_half(0)
+        y_g = single(t, 1, 0, N_TILE)
+        squash(y_g[:], 1)
+        squash(cell[:, 1, :], 1)
+        y_c = product(nc.gpsimd, "y_cell", y_i[:], y_g[:])
+        finish_half(1)
+        y_o = single(t, 2, 0, N_TILE)
+        squash(y_o[:], 2)
+        squash(y_c[:], 1)
+        store(t, 0, N_TILE, product(nc.gpsimd, "y_hidden", y_o[:], y_c[:]))
+        t = t + 1
+        z_i = single(t, 0, 0, N_TILE)
+        squash(z_i[:], 0)
+        left_g = single(t, 1, 0, 256)
+        squash(left_g[:], 1)
+        right_g = single(t, 1, 256, 512)
+        squash(right_g[:], 1)
+        left_o = single(t, 2, 0, 256)
+        middle_o = single(t, 2, 256, 384)
+        squash(middle_o[:], 2)
+        squash(left_o[:], 2)
+        left_c = product(nc.vector, "piece_cell", z_i[:, 0:256], left_g[:])
+        squash(left_c[:], 1)
+        right_c = product(nc.vector, "piece_cell", z_i[:, 256:512], right_g[:])
+        squash(right_c[:], 1)
+        right_o = single(t, 2, 384, 512)
+        squash(right_o[:], 2)
+        store(t, 0, 256, product(nc.vector, "piece_hidden", left_o[:], left_c[:]))
+        store(t, 256, 384, product(nc.vector, "piece_hidden", middle_o[:], right_c[:, 0:128]))
+        store(t, 384, 512, product(nc.vector, "piece_hidden", right_o[:], right_c[:, 128:256]))

@@ -7,13 +7,16 @@ TOKENS, K, H = 1536, 2048, 1536
 P = 128
 K_PASS = 512
 PASSES = K // K_PASS
-X_CODE_PARTS = ((0, 256), (256, 768), (768, 1536))
-X_PLANE_PARTS = ((0, 768), (768, 1536))
+X_CODE_PARTS = ((0, 256), (256, 512), (512, 1536))
+X_PLANE_PARTS = ((0, 512), (512, 1536))
 W_PARTS = ((0, 512), (512, 1536))
 N_TILE = 512
 BLOCKS = H // N_TILE
+SUMS_BEHIND = (1, 3)
 GATES = (0, 2, 3)
 TOKEN_TILES = TOKENS // P
+BANKS = 8
+QUAD = 4
 QUADRANT = 32
 
 FLOPS = 2 * TOKENS * K * len(GATES) * H
@@ -65,7 +68,7 @@ def tile_lstmbaseline_pa_kernel(tc, x_words, x_scales, w_words, w_scales, b_ih, 
     with ExitStack() as ctx:
         keep = ctx.enter_context(tc.tile_pool(name="keep", bufs=1))
         work = ctx.enter_context(tc.tile_pool(name="work", bufs=3))
-        psum = ctx.enter_context(tc.psum_pool(name="psum", bufs=8))
+        psum = ctx.enter_context(tc.psum_pool(name="psum", bufs=1))
         ctx.enter_context(tc.manual_schedule())
 
         def codes_tile(label, columns):
@@ -112,23 +115,26 @@ def tile_lstmbaseline_pa_kernel(tc, x_words, x_scales, w_words, w_scales, b_ih, 
         load_scales(nc, w_planes[0][0], w_scales, GATES[0] * H)
         load_codes(nc, x_codes[0], x_words, 0, others)
         load_codes(nc, w_codes[0][0], w_words, GATES[0] * H, others)
+        load_codes(nc, x_codes[1], x_words, X_CODE_PARTS[1][0], range(PASSES))
         for j in (1, 2):
             load_scales(nc, w_planes[j][0], w_scales, GATES[j] * H)
             load_codes(nc, w_codes[j][0], w_words, GATES[j] * H, range(PASSES))
-        load_codes(nc, x_codes[1], x_words, X_CODE_PARTS[1][0], range(PASSES))
         load_scales(nc, x_planes[1], x_scales, X_PLANE_PARTS[1][0])
         load_codes(nc, x_codes[2], x_words, X_CODE_PARTS[2][0], range(PASSES))
-        for j, gate in enumerate(GATES):
-            load_scales(nc, w_planes[j][1], w_scales, gate * H + N_TILE)
-            load_codes(nc, w_codes[j][1], w_words, gate * H + N_TILE, range(PASSES))
         for j, gate in enumerate(GATES):
             for s, vector in enumerate((b_ih, b_hh)):
                 nc.sync.dma_start(
                     out=spread[s][:, j, :], in_=vector[gate * H + N_TILE : (gate + 1) * H].partition_broadcast(P)
                 )
+        for j, gate in enumerate(GATES):
+            load_scales(nc, w_planes[j][1], w_scales, gate * H + N_TILE)
+            load_codes(nc, w_codes[j][1], w_words, gate * H + N_TILE, range(PASSES))
+
+        def bank_tile(bank, width=N_TILE):
+            return psum.tile([P, width], F32, name="bank%d" % bank)
 
         for j in range(len(GATES)):
-            acc = psum.tile([P, N_TILE], F32, name="acc")
+            acc = bank_tile(BANKS - 1 - j)
             for s in range(2):
                 nc.tensor.matmul(
                     out=acc[:], lhsT=ones[:, j, :], rhs=bias_rows[:, s, :], start=(s == 0), stop=(s == 1)
@@ -164,15 +170,14 @@ def tile_lstmbaseline_pa_kernel(tc, x_words, x_scales, w_words, w_scales, b_ih, 
             nc.vector.tensor_tensor(out=out_ap, in0=acc[:], in1=bias(c, j, n0, n1), op=ADD)
 
         rest_sums = [(c, j) for c in range(1, BLOCKS) for j in range(len(GATES))]
-        pairs = [(c, t0) for c in range(BLOCKS) for t0 in range(0, TOKEN_TILES, 2)]
 
-        def gate_pair(c, t0, j):
-            accs = [psum.tile([P, N_TILE], F32, name="acc") for u in range(2)]
+        def gate_pair(c, t0, j, banks, order=(0, 1)):
+            accs = [bank_tile(banks[u]) for u in range(2)]
             for g in range(PASSES):
-                for u in range(2):
+                for u in order:
                     multiply(accs[u], t0 + u, c, j, g)
             zj = work.tile([P, 2, N_TILE], F32, name="z%d" % j)
-            for u in range(2):
+            for u in order:
                 add_bias(zj[:, u, :], accs[u], c, j)
             return zj
 
@@ -183,52 +188,60 @@ def tile_lstmbaseline_pa_kernel(tc, x_words, x_scales, w_words, w_scales, b_ih, 
             engine.tensor_tensor(out=result, in0=a, in1=b, op=MULT)
 
         def finish(c, t0, cell, out_gate):
-            hidden = work.tile([P, 2, N_TILE], F32, name="hidden")
+            hidden = work.tile([P, 2, N_TILE], F32, name="hidden", bufs=5)
             multiply_into(nc.vector, hidden[:], out_gate[:], cell[:])
             nc.sync.dma_start(
                 out=out[P * t0 : P * (t0 + 2), c * N_TILE : (c + 1) * N_TILE].rearrange("(u p) n -> p u n", p=P),
                 in_=hidden[:],
             )
 
-        waiting = None
-        for c, t0 in pairs[:-2]:
-            in_gate = gate_pair(c, t0, 0)
-            squash(in_gate[:], 0)
-            if waiting:
-                squash(waiting[2][:], 1)
-            cell_gate = gate_pair(c, t0, 1)
-            squash(cell_gate[:], 1)
-            if waiting:
-                finish(*waiting)
-            cell = work.tile([P, 2, N_TILE], F32, name="cell")
-            multiply_into(nc.gpsimd, cell[:], in_gate[:], cell_gate[:])
-            out_gate = gate_pair(c, t0, 2)
-            squash(out_gate[:], 2)
-            waiting = (c, t0, cell, out_gate)
-            if t0 >= 4 and rest_sums:
-                bc, bj = rest_sums[0]
-                rest_sums = rest_sums[1:]
-                part = slice((bc - 1) * N_TILE, bc * N_TILE)
-                nc.gpsimd.tensor_tensor(
-                    out=bias_rest[:, bj, part], in0=spread[0][:, bj, part], in1=spread[1][:, bj, part], op=ADD
-                )
+        quads = [(c, t0) for c in range(BLOCKS) for t0 in range(0, TOKEN_TILES, QUAD)]
+        use = 0
+        waiting = []
+        for number, (c, t0) in enumerate(quads[:-1]):
+            z = [[None, None] for j in range(len(GATES))]
+            cells = [None, None]
+            for j in range(len(GATES)):
+                first_bank = QUAD * (use % 2)
+                order = (0, 1) if use // 2 % 2 == 0 else (1, 0)
+                use += 1
+                for turn, v in enumerate(order):
+                    banks = (first_bank + 2 * v, first_bank + 2 * v + 1)
+                    z[j][v] = gate_pair(c, t0 + 2 * v, j, banks, order)
+                    squash(z[j][v][:], j)
+                    if j == 0 and waiting:
+                        finish(*waiting[turn])
+                    if j == 2:
+                        squash(cells[v][:], 1)
+                    if j == 1:
+                        cells[v] = work.tile([P, 2, N_TILE], F32, name="cell")
+                        multiply_into(nc.gpsimd, cells[v][:], z[0][v][:], z[1][v][:])
+            waiting = [(c, t0 + 2 * v, cells[v], z[2][v]) for v in order]
+            for bc, bj in rest_sums:
+                if number == SUMS_BEHIND[bc - 1]:
+                    part = slice((bc - 1) * N_TILE, bc * N_TILE)
+                    nc.gpsimd.tensor_tensor(
+                        out=bias_rest[:, bj, part], in0=spread[0][:, bj, part], in1=spread[1][:, bj, part], op=ADD
+                    )
 
-        c, t0 = pairs[-2]
-        in_gate = gate_pair(c, t0, 0)
+        c, t0 = quads[-1]
+        banks = [QUAD * (use % 2) + b for b in range(QUAD)]
+        banks = banks + [(b + QUAD) % BANKS for b in banks]
+        in_gate = gate_pair(c, t0, 0, banks[0:2])
         for u in range(2):
             squash(in_gate[:, u, :], 0)
-        squash(waiting[2][:], 1)
-        cell_gate = gate_pair(c, t0, 1)
+        finish(*waiting[0])
+        cell_gate = gate_pair(c, t0, 1, banks[2:4])
+        finish(*waiting[1])
         cell = work.tile([P, 2, N_TILE], F32, name="cell")
         for u in range(2):
             squash(cell_gate[:, u, :], 1)
             multiply_into(nc.gpsimd, cell[:, u, :], in_gate[:, u, :], cell_gate[:, u, :])
-        finish(*waiting)
-        out_gate = gate_pair(c, t0, 2)
+        out_gate = gate_pair(c, t0, 2, banks[4:6])
         squash(cell[:, 0, :], 1)
         for u in range(2):
             squash(out_gate[:, u, :], 2)
-        hidden = work.tile([P, 2, N_TILE], F32, name="hidden")
+        hidden = work.tile([P, 2, N_TILE], F32, name="hidden", bufs=5)
 
         def finish_half(u):
             multiply_into(nc.gpsimd, hidden[:, u, :], out_gate[:, u, :], cell[:, u, :])
@@ -238,8 +251,8 @@ def tile_lstmbaseline_pa_kernel(tc, x_words, x_scales, w_words, w_scales, b_ih, 
 
         t = TOKEN_TILES - 2
 
-        def single(t, j, n0, n1):
-            acc = psum.tile([P, n1 - n0], F32, name="acc")
+        def single(t, j, n0, n1, bank):
+            acc = bank_tile(bank, n1 - n0)
             for g in range(PASSES):
                 multiply(acc, t, c, j, g, n0)
             piece = work.tile([P, n1 - n0], F32, name="piece%d" % j)
@@ -254,34 +267,34 @@ def tile_lstmbaseline_pa_kernel(tc, x_words, x_scales, w_words, w_scales, b_ih, 
         def store(t, n0, n1, result):
             nc.sync.dma_start(out=out[P * t : P * (t + 1), c * N_TILE + n0 : c * N_TILE + n1], in_=result[:])
 
-        y_i = single(t, 0, 0, N_TILE)
+        y_i = single(t, 0, 0, N_TILE, banks[6])
         squash(y_i[:], 0)
         finish_half(0)
-        y_g = single(t, 1, 0, N_TILE)
+        y_g = single(t, 1, 0, N_TILE, banks[7])
         squash(y_g[:], 1)
         squash(cell[:, 1, :], 1)
         y_c = product(nc.gpsimd, "y_cell", y_i[:], y_g[:])
         finish_half(1)
-        y_o = single(t, 2, 0, N_TILE)
+        y_o = single(t, 2, 0, N_TILE, banks[0])
         squash(y_o[:], 2)
         squash(y_c[:], 1)
         store(t, 0, N_TILE, product(nc.gpsimd, "y_hidden", y_o[:], y_c[:]))
         t = t + 1
-        z_i = single(t, 0, 0, N_TILE)
+        z_i = single(t, 0, 0, N_TILE, banks[1])
         squash(z_i[:], 0)
-        left_g = single(t, 1, 0, 256)
+        left_g = single(t, 1, 0, 256, banks[2])
         squash(left_g[:], 1)
-        right_g = single(t, 1, 256, 512)
+        right_g = single(t, 1, 256, 512, banks[3])
         squash(right_g[:], 1)
-        left_o = single(t, 2, 0, 256)
-        middle_o = single(t, 2, 256, 384)
+        left_o = single(t, 2, 0, 256, banks[4])
+        middle_o = single(t, 2, 256, 384, banks[5])
         squash(middle_o[:], 2)
         squash(left_o[:], 2)
         left_c = product(nc.vector, "piece_cell", z_i[:, 0:256], left_g[:])
         squash(left_c[:], 1)
         right_c = product(nc.vector, "piece_cell", z_i[:, 256:512], right_g[:])
         squash(right_c[:], 1)
-        right_o = single(t, 2, 384, 512)
+        right_o = single(t, 2, 384, 512, banks[6])
         squash(right_o[:], 2)
         store(t, 0, 256, product(nc.vector, "piece_hidden", left_o[:], left_c[:]))
         store(t, 256, 384, product(nc.vector, "piece_hidden", middle_o[:], right_c[:, 0:128]))

@@ -19,6 +19,8 @@ BANKS = 8
 QUAD = 4
 QUADRANT = 32
 
+LEAD_X_CODES, LEAD_X_PLANES, LEAD_W_CODES, LEAD_W_PLANES = 0, 64, 128, 192
+
 FLOPS = 2 * TOKENS * K * len(GATES) * H
 BYTES = (
     K * TOKENS // 2 + K // 32 * TOKENS
@@ -71,16 +73,20 @@ def tile_lstmbaseline_pa_kernel(tc, x_words, x_scales, w_words, w_scales, b_ih, 
         psum = ctx.enter_context(tc.psum_pool(name="psum", bufs=1))
         ctx.enter_context(tc.manual_schedule())
 
-        def codes_tile(label, columns):
-            return keep.tile([P, PASSES, 2 * columns], U8, align_bytes=256, name=label + "_codes")
+        def operand_tile(label, width, lead):
+            tile = keep.tile([P, lead + PASSES * width], U8, align_bytes=256, name=label)
+            return tile[:, lead:].rearrange("p (g n) -> p g n", g=PASSES)
 
-        def planes_tile(label, columns):
-            return keep.tile([P, PASSES, columns], U8, align_bytes=256, name=label + "_planes")
+        def tiles(label, parts, bytes_a_column, lead):
+            return [
+                operand_tile("%s%d" % (label, s), bytes_a_column * (stop - start), lead)
+                for s, (start, stop) in enumerate(parts)
+            ]
 
-        x_codes = [codes_tile("x%d" % s, stop - start) for s, (start, stop) in enumerate(X_CODE_PARTS)]
-        x_planes = [planes_tile("x%d" % s, stop - start) for s, (start, stop) in enumerate(X_PLANE_PARTS)]
-        w_codes = [[codes_tile("w%d%d" % (j, s), b - a) for s, (a, b) in enumerate(W_PARTS)] for j in range(3)]
-        w_planes = [[planes_tile("w%d%d" % (j, s), b - a) for s, (a, b) in enumerate(W_PARTS)] for j in range(3)]
+        x_codes = tiles("x_codes", X_CODE_PARTS, 2, LEAD_X_CODES)
+        x_planes = tiles("x_planes", X_PLANE_PARTS, 1, LEAD_X_PLANES)
+        w_codes = [tiles("w_codes%d" % j, W_PARTS, 2, LEAD_W_CODES) for j in range(len(GATES))]
+        w_planes = [tiles("w_planes%d" % j, W_PARTS, 1, LEAD_W_PLANES) for j in range(len(GATES))]
 
         bias_rows = keep.tile([P, 2, N_TILE], BF16, name="bias_rows")
         ones = keep.tile([P, len(GATES), P], BF16, name="ones")
@@ -89,12 +95,12 @@ def tile_lstmbaseline_pa_kernel(tc, x_words, x_scales, w_words, w_scales, b_ih, 
         spread = [keep.tile([P, len(GATES), H - N_TILE], BF16, name="spread%d" % s) for s in range(2)]
         warm = keep.tile([P, 1], F32, name="warm")
 
-        nc.vector.memset(x_planes[0][:].bitcast(I32), 0)
-        nc.vector.memset(w_planes[0][0][:].bitcast(I32), 0)
+        nc.vector.memset(x_planes[0].bitcast(I32), 0)
+        nc.vector.memset(w_planes[0][0].bitcast(I32), 0)
         nc.vector.memset(warm[:], 0.0)
-        nc.vector.memset(w_planes[1][0][:].bitcast(I32), 0)
-        nc.vector.memset(w_planes[2][0][:].bitcast(I32), 0)
-        nc.vector.memset(x_planes[1][:].bitcast(I32), 0)
+        nc.vector.memset(w_planes[1][0].bitcast(I32), 0)
+        nc.vector.memset(w_planes[2][0].bitcast(I32), 0)
+        nc.vector.memset(x_planes[1].bitcast(I32), 0)
 
         nc.gpsimd.memset(bias_rows[:].rearrange("p s n -> p (s n)").bitcast(F32), 0.0)
         for s, vector in enumerate((b_ih, b_hh)):
@@ -106,7 +112,7 @@ def tile_lstmbaseline_pa_kernel(tc, x_words, x_scales, w_words, w_scales, b_ih, 
             nc.gpsimd.memset(ones[QUADRANT * gate : QUADRANT * (gate + 1), j, :], 1.0)
         nc.gpsimd.memset(bias_rows[QUADRANT : 2 * QUADRANT, :, :].rearrange("p s n -> p (s n)").bitcast(F32), 0.0)
         for j in range(len(GATES)):
-            nc.gpsimd.memset(w_planes[j][1][:].bitcast(F32), 0.0)
+            nc.gpsimd.memset(w_planes[j][1].bitcast(F32), 0.0)
 
         first, others = range(0, 1), range(1, PASSES)
         load_codes(nc, w_codes[0][0], w_words, GATES[0] * H, first)

from contextlib import ExitStack

import concourse.mybir as mybir

TOKENS, K, H = 1536, 2048, 1536

P = 128
K_PASS = 512
PASSES = K // K_PASS
X_CODE_PARTS = ((0, 256), (256, 512), (512, 1536))
X_PLANE_PARTS = ((0, 512), (512, 1536))
W_PARTS = ((0, 512), (512, 1536))
N_TILE = 512
BLOCKS = H // N_TILE
SUMS_BEHIND = (1, 3)
GATES = (0, 2, 3)
TOKEN_TILES = TOKENS // P
BANKS = 8
QUAD = 4
QUADRANT = 32

LEAD_X_CODES, LEAD_X_PLANES, LEAD_W_CODES, LEAD_W_PLANES = 0, 64, 128, 192

FLOPS = 2 * TOKENS * K * len(GATES) * H
BYTES = (
    K * TOKENS // 2 + K // 32 * TOKENS
    + K * len(GATES) * H // 2 + K // 32 * len(GATES) * H
    + 2 * 2 * len(GATES) * H
    + 4 * TOKENS * H
)

F32 = mybir.dt.float32
BF16 = mybir.dt.bfloat16
I32 = mybir.dt.int32
U8 = mybir.dt.uint8
FP4X4 = mybir.dt.float4_e2m1fn_x4
ADD = mybir.AluOpType.add
MULT = mybir.AluOpType.mult
SIGMOID = mybir.ActivationFunctionType.Sigmoid
TANH = mybir.ActivationFunctionType.Tanh


def load_codes(nc, codes, words, first_column, passes):
    width = codes.shape[2]
    source = words[passes.start : passes.stop, :, 2 * first_column : 2 * first_column + width]
    nc.sync.dma_start(
        out=codes[:, passes.start : passes.stop, :].bitcast(I32),
        in_=source.rearrange("g p n -> p g n").bitcast(I32),
    )


def load_scales(nc, planes, scales, first_column):
    width = planes.shape[2]
    for q in range(4):
        source = scales[:, 4 * q : 4 * q + 4, first_column : first_column + width]
        nc.sync.dma_start(
            out=planes[QUADRANT * q : QUADRANT * q + 4, :, :].bitcast(I32),
            in_=source.rearrange("g r n -> r g n").bitcast(I32),
        )


def part_of(tiles, parts, column):
    for tile, (start, stop) in zip(tiles, parts):
        if start <= column < stop:
            return tile, column - start


def tile_lstmbaseline_pa_kernel(tc, x_words, x_scales, w_words, w_scales, b_ih, b_hh, out):
    nc = tc.nc
    with ExitStack() as ctx:
        keep = ctx.enter_context(tc.tile_pool(name="keep", bufs=1))
        work = ctx.enter_context(tc.tile_pool(name="work", bufs=3))
        psum = ctx.enter_context(tc.psum_pool(name="psum", bufs=1))
        ctx.enter_context(tc.manual_schedule())

        def operand_tile(label, width, lead):
            tile = keep.tile([P, lead + PASSES * width], U8, align_bytes=256, name=label)
            return tile[:, lead:].rearrange("p (g n) -> p g n", g=PASSES)

        def tiles(label, parts, bytes_a_column, lead):
            return [
                operand_tile("%s%d" % (label, s), bytes_a_column * (stop - start), lead)
                for s, (start, stop) in enumerate(parts)
            ]

        x_codes = tiles("x_codes", X_CODE_PARTS, 2, LEAD_X_CODES)
        x_planes = tiles("x_planes", X_PLANE_PARTS, 1, LEAD_X_PLANES)
        w_codes = [tiles("w_codes%d" % j, W_PARTS, 2, LEAD_W_CODES) for j in range(len(GATES))]
        w_planes = [tiles("w_planes%d" % j, W_PARTS, 1, LEAD_W_PLANES) for j in range(len(GATES))]

        bias_rows = keep.tile([P, 2, N_TILE], BF16, name="bias_rows")
        ones = keep.tile([P, len(GATES), P], BF16, name="ones")
        bias_head = keep.tile([P, len(GATES), N_TILE], F32, name="bias_head")
        bias_rest = keep.tile([P, len(GATES), H - N_TILE], F32, name="bias_rest")
        spread = [keep.tile([P, len(GATES), H - N_TILE], BF16, name="spread%d" % s) for s in range(2)]
        warm = keep.tile([P, 1], F32, name="warm")

        nc.vector.memset(x_planes[0].bitcast(I32), 0)
        nc.vector.memset(w_planes[0][0].bitcast(I32), 0)
        nc.vector.memset(warm[:], 0.0)
        nc.vector.memset(w_planes[1][0].bitcast(I32), 0)
        nc.vector.memset(w_planes[2][0].bitcast(I32), 0)
        nc.vector.memset(x_planes[1].bitcast(I32), 0)

        nc.gpsimd.memset(bias_rows[:].rearrange("p s n -> p (s n)").bitcast(F32), 0.0)
        for s, vector in enumerate((b_ih, b_hh)):
            rows = vector.rearrange("(g n) -> g n", g=4)
            nc.scalar.dma_start(out=bias_rows[0:P:QUADRANT, s, :], in_=rows[:, 0:N_TILE])
        nc.scalar.activation(warm[:], warm[:], SIGMOID)
        nc.gpsimd.memset(ones[:], 0.0)
        for j, gate in enumerate(GATES):
            nc.gpsimd.memset(ones[QUADRANT * gate : QUADRANT * (gate + 1), j, :], 1.0)
        nc.gpsimd.memset(bias_rows[QUADRANT : 2 * QUADRANT, :, :].rearrange("p s n -> p (s n)").bitcast(F32), 0.0)
        for j in range(len(GATES)):
            nc.gpsimd.memset(w_planes[j][1].bitcast(F32), 0.0)

        first, others = range(0, 1), range(1, PASSES)
        load_codes(nc, w_codes[0][0], w_words, GATES[0] * H, first)
        load_codes(nc, x_codes[0], x_words, 0, first)
        load_scales(nc, x_planes[0], x_scales, 0)
        load_scales(nc, w_planes[0][0], w_scales, GATES[0] * H)
        load_codes(nc, x_codes[0], x_words, 0, others)
        load_codes(nc, w_codes[0][0], w_words, GATES[0] * H, others)
        load_codes(nc, x_codes[1], x_words, X_CODE_PARTS[1][0], range(PASSES))
        for j in (1, 2):
            load_scales(nc, w_planes[j][0], w_scales, GATES[j] * H)
            load_codes(nc, w_codes[j][0], w_words, GATES[j] * H, range(PASSES))
        load_scales(nc, x_planes[1], x_scales, X_PLANE_PARTS[1][0])
        load_codes(nc, x_codes[2], x_words, X_CODE_PARTS[2][0], range(PASSES))
        for j, gate in enumerate(GATES):
            for s, vector in enumerate((b_ih, b_hh)):
                nc.sync.dma_start(
                    out=spread[s][:, j, :], in_=vector[gate * H + N_TILE : (gate + 1) * H].partition_broadcast(P)
                )
        for j, gate in enumerate(GATES):
            load_scales(nc, w_planes[j][1], w_scales, gate * H + N_TILE)
            load_codes(nc, w_codes[j][1], w_words, gate * H + N_TILE, range(PASSES))

        def bank_tile(bank, width=N_TILE):
            return psum.tile([P, width], F32, name="bank%d" % bank)

        for j in range(len(GATES)):
            acc = bank_tile(BANKS - 1 - j)
            for s in range(2):
                nc.tensor.matmul(
                    out=acc[:], lhsT=ones[:, j, :], rhs=bias_rows[:, s, :], start=(s == 0), stop=(s == 1)
                )
            if j == 1:
                nc.vector.tensor_copy(out=bias_head[:, j, :], in_=acc[:])
            else:
                nc.scalar.copy(bias_head[:, j, :], acc[:])

        def bias(c, j, n0=0, n1=N_TILE):
            if c == 0:
                return bias_head[:, j, n0:n1]
            first_column = (c - 1) * N_TILE
            return bias_rest[:, j, first_column + n0 : first_column + n1]

        def multiply(acc, t, c, j, g, column=0):
            width = acc.shape[1]
            x_code, m0 = part_of(x_codes, X_CODE_PARTS, P * t)
            x_plane, m1 = part_of(x_planes, X_PLANE_PARTS, P * t)
            w_code, n0 = part_of(w_codes[j], W_PARTS, N_TILE * c + column)
            w_plane, n1 = part_of(w_planes[j], W_PARTS, N_TILE * c + column)
            nc.tensor.matmul_mx(
                out=acc[:],
                lhsT=x_code[:, g, 2 * m0 : 2 * (m0 + P)].bitcast(FP4X4),
                lhsT_scale=x_plane[:, g, m1 : m1 + P],
                rhs=w_code[:, g, 2 * n0 : 2 * (n0 + width)].bitcast(FP4X4),
                rhs_scale=w_plane[:, g, n1 : n1 + width],
                start=(g == 0),
                stop=(g == PASSES - 1),
            )

        def add_bias(out_ap, acc, c, j, n0=0, n1=N_TILE):
            nc.vector.tensor_tensor(out=out_ap, in0=acc[:], in1=bias(c, j, n0, n1), op=ADD)

        rest_sums = [(c, j) for c in range(1, BLOCKS) for j in range(len(GATES))]

        def gate_pair(c, t0, j, banks, order=(0, 1)):
            accs = [bank_tile(banks[u]) for u in range(2)]
            for g in range(PASSES):
                for u in order:
                    multiply(accs[u], t0 + u, c, j, g)
            zj = work.tile([P, 2, N_TILE], F32, name="z%d" % j)
            for u in order:
                add_bias(zj[:, u, :], accs[u], c, j)
            return zj

        def squash(ap, j):
            nc.scalar.activation(ap, ap, TANH if j == 1 else SIGMOID)

        def multiply_into(engine, result, a, b):
            engine.tensor_tensor(out=result, in0=a, in1=b, op=MULT)

        def finish(c, t0, cell, out_gate):
            hidden = work.tile([P, 2, N_TILE], F32, name="hidden", bufs=5)
            multiply_into(nc.vector, hidden[:], out_gate[:], cell[:])
            nc.sync.dma_start(
                out=out[P * t0 : P * (t0 + 2), c * N_TILE : (c + 1) * N_TILE].rearrange("(u p) n -> p u n", p=P),
                in_=hidden[:],
            )

        quads = [(c, t0) for c in range(BLOCKS) for t0 in range(0, TOKEN_TILES, QUAD)]
        use = 0
        waiting = []
        for number, (c, t0) in enumerate(quads[:-1]):
            z = [[None, None] for j in range(len(GATES))]
            cells = [None, None]
            for j in range(len(GATES)):
                first_bank = QUAD * (use % 2)
                order = (0, 1) if use // 2 % 2 == 0 else (1, 0)
                use += 1
                for turn, v in enumerate(order):
                    banks = (first_bank + 2 * v, first_bank + 2 * v + 1)
                    z[j][v] = gate_pair(c, t0 + 2 * v, j, banks, order)
                    squash(z[j][v][:], j)
                    if j == 0 and waiting:
                        finish(*waiting[turn])
                    if j == 2:
                        squash(cells[v][:], 1)
                    if j == 1:
                        cells[v] = work.tile([P, 2, N_TILE], F32, name="cell")
                        multiply_into(nc.gpsimd, cells[v][:], z[0][v][:], z[1][v][:])
            waiting = [(c, t0 + 2 * v, cells[v], z[2][v]) for v in order]
            for bc, bj in rest_sums:
                if number == SUMS_BEHIND[bc - 1]:
                    part = slice((bc - 1) * N_TILE, bc * N_TILE)
                    nc.gpsimd.tensor_tensor(
                        out=bias_rest[:, bj, part], in0=spread[0][:, bj, part], in1=spread[1][:, bj, part], op=ADD
                    )

        c, t0 = quads[-1]
        banks = [QUAD * (use % 2) + b for b in range(QUAD)]
        banks = banks + [(b + QUAD) % BANKS for b in banks]
        in_gate = gate_pair(c, t0, 0, banks[0:2])
        for u in range(2):
            squash(in_gate[:, u, :], 0)
        finish(*waiting[0])
        cell_gate = gate_pair(c, t0, 1, banks[2:4])
        finish(*waiting[1])
        cell = work.tile([P, 2, N_TILE], F32, name="cell")
        for u in range(2):
            squash(cell_gate[:, u, :], 1)
            multiply_into(nc.gpsimd, cell[:, u, :], in_gate[:, u, :], cell_gate[:, u, :])
        out_gate = gate_pair(c, t0, 2, banks[4:6])
        squash(cell[:, 0, :], 1)
        for u in range(2):
            squash(out_gate[:, u, :], 2)
        hidden = work.tile([P, 2, N_TILE], F32, name="hidden", bufs=5)

        def finish_half(u):
            multiply_into(nc.gpsimd, hidden[:, u, :], out_gate[:, u, :], cell[:, u, :])
            nc.sync.dma_start(
                out=out[P * (t0 + u) : P * (t0 + u + 1), c * N_TILE : (c + 1) * N_TILE], in_=hidden[:, u, :]
            )

        t = TOKEN_TILES - 2

        def single(t, j, n0, n1, bank):
            acc = bank_tile(bank, n1 - n0)
            for g in range(PASSES):
                multiply(acc, t, c, j, g, n0)
            piece = work.tile([P, n1 - n0], F32, name="piece%d" % j)
            add_bias(piece[:], acc, c, j, n0, n1)
            return piece

        def product(engine, label, a, b):
            result = work.tile([P, a.shape[1]], F32, name=label)
            engine.tensor_tensor(out=result[:], in0=a, in1=b, op=MULT)
            return result

        def store(t, n0, n1, result):
            nc.sync.dma_start(out=out[P * t : P * (t + 1), c * N_TILE + n0 : c * N_TILE + n1], in_=result[:])

        y_i = single(t, 0, 0, N_TILE, banks[6])
        squash(y_i[:], 0)
        finish_half(0)
        y_g = single(t, 1, 0, N_TILE, banks[7])
        squash(y_g[:], 1)
        squash(cell[:, 1, :], 1)
        y_c = product(nc.gpsimd, "y_cell", y_i[:], y_g[:])
        finish_half(1)
        y_o = single(t, 2, 0, N_TILE, banks[0])
        squash(y_o[:], 2)
        squash(y_c[:], 1)
        store(t, 0, N_TILE, product(nc.gpsimd, "y_hidden", y_o[:], y_c[:]))
        t = t + 1
        z_i = single(t, 0, 0, N_TILE, banks[1])
        squash(z_i[:], 0)
        left_g = single(t, 1, 0, 256, banks[2])
        squash(left_g[:], 1)
        right_g = single(t, 1, 256, 512, banks[3])
        squash(right_g[:], 1)
        left_o = single(t, 2, 0, 256, banks[4])
        middle_o = single(t, 2, 256, 384, banks[5])
        squash(middle_o[:], 2)
        squash(left_o[:], 2)
        left_c = product(nc.vector, "piece_cell", z_i[:, 0:256], left_g[:])
        squash(left_c[:], 1)
        right_c = product(nc.vector, "piece_cell", z_i[:, 256:512], right_g[:])
        squash(right_c[:], 1)
        right_o = single(t, 2, 384, 512, banks[6])
        squash(right_o[:], 2)
        store(t, 0, 256, product(nc.vector, "piece_hidden", left_o[:], left_c[:]))
        store(t, 256, 384, product(nc.vector, "piece_hidden", middle_o[:], right_c[:, 0:128]))
        store(t, 384, 512, product(nc.vector, "piece_hidden", right_o[:], right_c[:, 128:256]))
